import numpy as np
import ml_dtypes


def mxq(x, axis, fmt="e4m3"):
    dtype, down = {"e4m3": (ml_dtypes.float8_e4m3fn, 7), "e5m2": (ml_dtypes.float8_e5m2, 14)}[fmt]
    v = np.moveaxis(np.asarray(x, np.float32).astype(ml_dtypes.bfloat16).astype(np.float64), axis, -1)
    blocks = v.reshape(v.shape[:-1] + (-1, 32))
    amax = np.abs(blocks).max(-1, keepdims=True)
    byte = np.maximum(np.where(amax > 0, np.frexp(amax)[1] - 1 + 127, 0) - down, 1)
    scale = np.exp2(byte - 127.0)
    codes = (blocks / scale).astype(np.float32).astype(dtype).astype(np.float64)
    return np.moveaxis((codes * scale).reshape(v.shape), -1, axis)


WIDE = False


def mx_kscale(k):
    if not WIDE:
        return np.ones(k)
    levels = np.array([10, -10, 5, -5, 0])
    if k % 512:
        return np.exp2(np.random.permutation(np.resize(levels, k // 32))).repeat(32)
    a = np.empty((k // 512, 16))
    for p in range(k // 512):
        a[p, :8] = np.random.permutation(np.resize(levels, 8))
        for g in range(8):
            far = levels[np.abs(levels - a[p, g]) >= 10]
            a[p, g + 8] = far[np.random.randint(len(far))]
    return np.exp2(a.ravel()).repeat(32)


BF16 = ml_dtypes.bfloat16


def bf(x):
    return np.asarray(x, np.float32).astype(BF16)


def f64(x):
    return np.asarray(x).astype(np.float64)


B, C, H, W, F, KH, KW = 8, 512, 18, 16, 128, 3, 3
K = KH * KW * C
SPARSITY = 0.7


def extract_patches(x, kh, kw):
    bb, s1, s2, cc = x.shape
    o1, o2 = s1 - kh + 1, s2 - kw + 1
    pats = np.stack([x[:, i:i + o1, j:j + o2, :] for i in range(kh) for j in range(kw)], axis=3)
    return pats.reshape(bb, o1, o2, kh * kw * cc)


def setup_inputs():
    s = mx_kscale(C)
    limit = np.sqrt(6.0 / (F + K))
    vals = np.random.uniform(-limit, limit, (F, K))
    mask = np.random.random((F, K)) >= SPARSITY
    mask[:, ::32] = True
    return {"inputs": bf(np.random.standard_normal((B, C, H, W)) * s[None, :, None, None]),
            "kernel": bf(vals * mask / np.tile(s, KH * KW)[None, :])}


def reference(inputs, kernel):
    x = np.transpose(f64(inputs), (0, 3, 2, 1))
    p = extract_patches(x, KH, KW)
    p2 = np.ascontiguousarray(p.reshape(-1, K))
    wt = np.ascontiguousarray(f64(kernel).T)
    out = mxq(p2, 1, "e4m3") @ mxq(wt, 0, "e4m3")
    return out.reshape(p.shape[:3] + (F,)).transpose(0, 3, 1, 2)

@@ -1,0 +1,192 @@
+import concourse.mybir as mybir
+from concourse.masks import make_identity
+
+F32 = mybir.dt.float32
+BF16 = mybir.dt.bfloat16
+I32 = mybir.dt.int32
+U32 = mybir.dt.uint32
+U8 = mybir.dt.uint8
+FP8X4 = mybir.dt.float8_e4m3fn_x4
+ADD = mybir.AluOpType.add
+
+P = 128
+B, C, H, W, F = 8, 512, 18, 16, 128
+KH, KW = 3, 3
+OA, OD = W - KH + 1, H - KW + 1
+GB = 2
+NG = B // GB
+ROW = GB * W
+N = OD * ROW
+NPASS = KH * KW
+
+FLOPS = 2 * B * OA * OD * KH * KW * C * F
+
+
+def tile_sparseconv2d_kernel(tc, inputs, kernel, out):
+    nc = tc.nc
+    with tc.tile_pool(name="keep", bufs=1) as keep, tc.psum_pool(name="psum", bufs=8) as psum, tc.manual_schedule():
+        ident = keep.tile([P, P], F32, name="ident")
+        make_identity(nc, ident[:])
+        xscales = keep.tile([P, NG, H * ROW], U8, name="xscales", align_bytes=64)
+        nc.vector.memset(xscales[:].rearrange("p g c -> p (g c)").bitcast(I32), 0)
+
+        kw = keep.tile([P, NPASS * C], BF16, name="kw")
+        raw = keep.tile([P, B, 4, H * W], BF16, name="raw")
+
+        def load_image(b):
+            nc.sync.dma_start(out=raw[:, b, :, :].rearrange("p t s -> p (t s)"), in_=inputs[b].rearrange("(p t) h w -> p (t h w)", t=4))
+
+        def load_weights(g0):
+            cols = slice(g0 * C, min(g0 + 2, NPASS) * C)
+            nc.sync.dma_start(out=kw[:, cols], in_=kernel[:, cols])
+
+        load_image(0)
+        load_image(1)
+        for g0 in range(0, NPASS, 2):
+            load_weights(g0)
+        for b in range(2, B):
+            load_image(b)
+
+        kwords = kw[:].bitcast(F32).rearrange("p (g q u) -> p g u q", q=P, u=2)
+        wgrp = keep.tile([P, NPASS * 4 * F], BF16, name="wgrp", align_bytes=64)
+        wgrp_words = wgrp[:].bitcast(F32).rearrange("p (g f u) -> p g f u", f=F, u=2)
+        wcodes = keep.tile([P, NPASS * F], U32, name="wcodes", align_bytes=64)
+        wscales = keep.tile([P, NPASS * F], U8, name="wscales", align_bytes=64)
+        grp = keep.tile([P, NG, H * ROW * 4], BF16, name="grp", align_bytes=64)
+        xcodes = keep.tile([P, NG, H * ROW], U32, name="xcodes", align_bytes=64)
+        xshift = keep.tile([P, NG, N], U8, name="xshift", align_bytes=64)
+        osb = keep.tile([P, NG, GB * OA * OD], F32, name="osb")
+        banks = {}
+
+        def regroup(b, engine, h0, h1):
+            dst = grp[:, b // GB, :].rearrange("p (h b w t) -> p h b w t", h=H, b=GB, w=W)[:, h0:h1, b % GB, :, :]
+            src = raw[:, b, :, h0 * W:h1 * W]
+            if engine == "v":
+                nc.vector.tensor_copy(
+                    out=dst.rearrange("p h (q i) t -> p h q t i", i=4),
+                    in_=src.rearrange("p t (h q i) -> p h q t i", q=4, i=4),
+                )
+            else:
+                nc.scalar.copy(out=dst, in_=src.rearrange("p t (h w) -> p h w t", w=W))
+
+        def quantise_image(g):
+            for h0, h1 in ((0, OD), (OD, H)):
+                nc.vector.quantize_mx(
+                    out=xcodes[:, g, h0 * ROW:h1 * ROW].bitcast(FP8X4),
+                    scales=xscales[:, g, h0 * ROW:h1 * ROW],
+                    in_=grp[:, g, h0 * ROW * 4:h1 * ROW * 4],
+                )
+            nc.vector.tensor_copy(out=xshift[:, g, :].bitcast(I32), in_=xscales[:, g, ROW:ROW + N].bitcast(I32))
+
+        def weights_transpose(g0, engine="s"):
+            n = min(2, NPASS - g0)
+            wt = psum.tile([P, 2, 2, F], F32, name="wt", tag="bank")
+            for k in range(n):
+                for u in range(2):
+                    nc.tensor.transpose(wt[:, k, u, :], kwords[:, g0 + k, u, :], ident[:])
+            if engine == "s":
+                nc.scalar.copy(out=wgrp_words[:, g0:g0 + n, :, :], in_=wt[:, 0:n, :, :].rearrange("p g u f -> p g f u"))
+            else:
+                nc.vector.tensor_copy(out=wgrp_words[:, g0:g0 + n, :, :], in_=wt[:, 0:n, :, :].rearrange("p g u f -> p g f u"))
+
+        def weights_quantise(g0):
+            n = min(2, NPASS - g0)
+            nc.vector.quantize_mx(
+                out=wcodes[:, g0 * F:(g0 + n) * F].bitcast(FP8X4),
+                scales=wscales[:, g0 * F:(g0 + n) * F],
+                in_=wgrp[:, g0 * 4 * F:(g0 + n) * 4 * F],
+            )
+
+        def multiply(g, i, d0=0, d1=OD):
+            n = (d1 - d0) * ROW
+            y = psum.tile([P, n], F32, name="y", tag="bank")
+            banks[(g, i, d0)] = y
+            for j in range(KW):
+                k = i * KW + j
+                c0 = (d0 + j) * ROW
+                plane = xshift[:, g, c0 - ROW:c0 - ROW + n] if j == 1 else xscales[:, g, c0:c0 + n]
+                nc.tensor.matmul_mx(
+                    out=y[:],
+                    lhsT=wcodes[:, k * F:(k + 1) * F].bitcast(FP8X4),
+                    lhsT_scale=wscales[:, k * F:(k + 1) * F],
+                    rhs=xcodes[:, g, c0:c0 + n].bitcast(FP8X4),
+                    rhs_scale=plane,
+                    start=(j == 0),
+                    stop=(j == KW - 1),
+                )
+
+        def multiply_shift_major(g):
+            ys = [psum.tile([P, N], F32, name="y%d" % i, tag="bank") for i in range(KH)]
+            for j in range(KW):
+                for i in range(KH):
+                    banks[(g, i, 0)] = ys[i]
+                    k = i * KW + j
+                    c0 = j * ROW
+                    plane = xshift[:, g, :] if j == 1 else xscales[:, g, c0:c0 + N]
+                    nc.tensor.matmul_mx(
+                        out=ys[i][:],
+                        lhsT=wcodes[:, k * F:(k + 1) * F].bitcast(FP8X4),
+                        lhsT_scale=wscales[:, k * F:(k + 1) * F],
+                        rhs=xcodes[:, g, c0:c0 + N].bitcast(FP8X4),
+                        rhs_scale=plane,
+                        start=(j == 0),
+                        stop=(j == KW - 1),
+                    )
+
+        def collect(g, i, d0=0, d1=OD):
+            src = banks[(g, i, d0)][:].rearrange("p (d b w) -> p b w d", d=d1 - d0, b=GB)[:, :, i:i + OA, :]
+            dst = osb[:, g, :].rearrange("p (b a d) -> p b a d", b=GB, a=OA)[:, :, :, d0:d1]
+            if i == 0:
+                nc.scalar.copy(out=dst, in_=src)
+            else:
+                nc.vector.tensor_tensor(out=dst, in0=src, in1=dst, op=ADD)
+
+        def store(g):
+            nc.sync.dma_start(
+                out=out[g * GB:(g + 1) * GB].rearrange("b f a d -> f b (a d)"),
+                in_=osb[:, g, :].rearrange("p (b s) -> p b s", b=GB),
+            )
+
+        regroup(0, "v", 0, H)
+        regroup(1, "v", 0, 12)
+        regroup(1, "s", 12, H)
+        quantise_image(0)
+        for g0 in (0, 2, 4):
+            weights_transpose(g0)
+            weights_quantise(g0)
+        weights_transpose(6)
+        regroup(2, "v", 0, H)
+        weights_quantise(6)
+        weights_transpose(8)
+        weights_quantise(8)
+        regroup(3, "s", 10, H)
+        regroup(3, "v", 0, 10)
+        for i in range(KH):
+            multiply(0, i)
+        quantise_image(1)
+        collect(0, 0)
+        regroup(4, "s", 0, H)
+        regroup(5, "v", 0, H)
+        multiply_shift_major(1)
+        regroup(6, "s", 0, H)
+        quantise_image(2)
+        collect(0, 1)
+        collect(0, 2)
+        store(0)
+        regroup(7, "s", 0, H)
+        collect(1, 0)
+        quantise_image(3)
+        for i in range(KH):
+            multiply(2, i)
+        collect(2, 0)
+        collect(1, 1)
+        collect(1, 2)
+        store(1)
+        collect(2, 1)
+        collect(2, 2)
+        store(2)
+        for d0 in (0, 8):
+            for i in range(KH):
+                multiply(3, i, d0, d0 + 8)
+                collect(3, i, d0, d0 + 8)
+        store(3)

@@ -18,6 +18,7 @@ NG = B // GB
 ROW = GB * W
 N = OD * ROW
 NPASS = KH * KW
+NWARM = 4
 
 FLOPS = 2 * B * OA * OD * KH * KW * C * F
 
@@ -25,6 +26,12 @@ FLOPS = 2 * B * OA * OD * KH * KW * C * F
 def tile_sparseconv2d_kernel(tc, inputs, kernel, out):
     nc = tc.nc
     with tc.tile_pool(name="keep", bufs=1) as keep, tc.psum_pool(name="psum", bufs=8) as psum, tc.manual_schedule():
+        zeros = keep.tile([P, N], BF16, name="zeros")
+        nc.vector.memset(zeros[:], 0.0)
+        warm = psum.tile([P, N], F32, name="warm", tag="bank")
+        for k in range(NWARM):
+            nc.tensor.matmul(warm[:], zeros[:, 0:P], zeros[:], start=True, stop=True)
+
         ident = keep.tile([P, P], F32, name="ident")
         make_identity(nc, ident[:])
         xscales = keep.tile([P, NG, H * ROW], U8, name="xscales", align_bytes=64)
@@ -41,10 +48,14 @@ def tile_sparseconv2d_kernel(tc, inputs, kernel, out):
             nc.sync.dma_start(out=kw[:, cols], in_=kernel[:, cols])
 
         load_image(0)
+        load_weights(0)
         load_image(1)
-        for g0 in range(0, NPASS, 2):
-            load_weights(g0)
-        for b in range(2, B):
+        load_weights(2)
+        load_weights(4)
+        load_weights(6)
+        load_image(2)
+        load_weights(8)
+        for b in range(3, B):
             load_image(b)
 
         kwords = kw[:].bitcast(F32).rearrange("p (g q u) -> p g u q", q=P, u=2)
@@ -69,13 +80,14 @@ def tile_sparseconv2d_kernel(tc, inputs, kernel, out):
             else:
                 nc.scalar.copy(out=dst, in_=src.rearrange("p t (h w) -> p h w t", w=W))
 
-        def quantise_image(g):
-            for h0, h1 in ((0, OD), (OD, H)):
-                nc.vector.quantize_mx(
-                    out=xcodes[:, g, h0 * ROW:h1 * ROW].bitcast(FP8X4),
-                    scales=xscales[:, g, h0 * ROW:h1 * ROW],
-                    in_=grp[:, g, h0 * ROW * 4:h1 * ROW * 4],
-                )
+        def quantise_rows(g, h0, h1):
+            nc.vector.quantize_mx(
+                out=xcodes[:, g, h0 * ROW:h1 * ROW].bitcast(FP8X4),
+                scales=xscales[:, g, h0 * ROW:h1 * ROW],
+                in_=grp[:, g, h0 * ROW * 4:h1 * ROW * 4],
+            )
+
+        def shift_scales(g):
             nc.vector.tensor_copy(out=xshift[:, g, :].bitcast(I32), in_=xscales[:, g, ROW:ROW + N].bitcast(I32))
 
         def weights_transpose(g0, engine="s"):
@@ -97,23 +109,26 @@ def tile_sparseconv2d_kernel(tc, inputs, kernel, out):
                 in_=wgrp[:, g0 * 4 * F:(g0 + n) * 4 * F],
             )
 
-        def multiply(g, i, d0=0, d1=OD):
+        def one_pass(g, k, d0=0, d1=OD):
+            i, j = divmod(k, KW)
             n = (d1 - d0) * ROW
-            y = psum.tile([P, n], F32, name="y", tag="bank")
-            banks[(g, i, d0)] = y
+            if j == 0:
+                banks[(g, i, d0)] = psum.tile([P, n], F32, name="y", tag="bank")
+            c0 = (d0 + j) * ROW
+            plane = xshift[:, g, c0 - ROW:c0 - ROW + n] if j == 1 else xscales[:, g, c0:c0 + n]
+            nc.tensor.matmul_mx(
+                out=banks[(g, i, d0)][:],
+                lhsT=wcodes[:, k * F:(k + 1) * F].bitcast(FP8X4),
+                lhsT_scale=wscales[:, k * F:(k + 1) * F],
+                rhs=xcodes[:, g, c0:c0 + n].bitcast(FP8X4),
+                rhs_scale=plane,
+                start=(j == 0),
+                stop=(j == KW - 1),
+            )
+
+        def multiply(g, i, d0=0, d1=OD):
             for j in range(KW):
-                k = i * KW + j
-                c0 = (d0 + j) * ROW
-                plane = xshift[:, g, c0 - ROW:c0 - ROW + n] if j == 1 else xscales[:, g, c0:c0 + n]
-                nc.tensor.matmul_mx(
-                    out=y[:],
-                    lhsT=wcodes[:, k * F:(k + 1) * F].bitcast(FP8X4),
-                    lhsT_scale=wscales[:, k * F:(k + 1) * F],
-                    rhs=xcodes[:, g, c0:c0 + n].bitcast(FP8X4),
-                    rhs_scale=plane,
-                    start=(j == 0),
-                    stop=(j == KW - 1),
-                )
+                one_pass(g, i * KW + j, d0, d1)
 
         def multiply_shift_major(g):
             ys = [psum.tile([P, N], F32, name="y%d" % i, tag="bank") for i in range(KH)]
@@ -147,46 +162,60 @@ def tile_sparseconv2d_kernel(tc, inputs, kernel, out):
                 in_=osb[:, g, :].rearrange("p (b s) -> p b s", b=GB),
             )
 
-        regroup(0, "v", 0, H)
-        regroup(1, "v", 0, 12)
-        regroup(1, "s", 12, H)
-        quantise_image(0)
-        for g0 in (0, 2, 4):
-            weights_transpose(g0)
-            weights_quantise(g0)
-        weights_transpose(6)
+        regroup(0, "s", 0, H)
+        regroup(1, "v", 0, H)
+        weights_transpose(0)
+        quantise_rows(0, 0, OD)
+        quantise_rows(0, OD, H)
+        weights_quantise(0)
+        shift_scales(0)
+        weights_transpose(2)
+        weights_quantise(2)
         regroup(2, "v", 0, H)
+        weights_transpose(4)
+        weights_quantise(4)
+        weights_transpose(6)
         weights_quantise(6)
         weights_transpose(8)
+        regroup(3, "s", 0, H)
         weights_quantise(8)
-        regroup(3, "s", 10, H)
-        regroup(3, "v", 0, 10)
         for i in range(KH):
             multiply(0, i)
-        quantise_image(1)
-        collect(0, 0)
-        regroup(4, "s", 0, H)
-        regroup(5, "v", 0, H)
+
+        quantise_rows(1, 0, OD)
+        quantise_rows(1, OD, H)
+        regroup(4, "v", 0, H)
+        shift_scales(1)
         multiply_shift_major(1)
-        regroup(6, "s", 0, H)
-        quantise_image(2)
+
+        regroup(5, "s", 0, H)
+        collect(0, 0)
+        regroup(6, "v", 0, H)
+        quantise_rows(2, 0, OD)
+        quantise_rows(2, OD, H)
         collect(0, 1)
+        shift_scales(2)
+        multiply_shift_major(2)
         collect(0, 2)
         store(0)
+
         regroup(7, "s", 0, H)
+        quantise_rows(3, 0, OD)
+        quantise_rows(3, OD, H)
         collect(1, 0)
-        quantise_image(3)
-        for i in range(KH):
-            multiply(2, i)
-        collect(2, 0)
+        shift_scales(3)
         collect(1, 1)
         collect(1, 2)
         store(1)
+
+        multiply(3, 0)
+        collect(2, 0)
         collect(2, 1)
         collect(2, 2)
         store(2)
-        for d0 in (0, 8):
-            for i in range(KH):
+        collect(3, 0)
+        for i in (1, 2):
+            for d0 in (0, 8):
                 multiply(3, i, d0, d0 + 8)
                 collect(3, i, d0, d0 + 8)
         store(3)

@@ -29,8 +29,12 @@ def tile_sparseconv2d_kernel(tc, inputs, kernel, out):
         zeros = keep.tile([P, N], BF16, name="zeros")
         nc.vector.memset(zeros[:], 0.0)
         warm = psum.tile([P, N], F32, name="warm", tag="bank")
-        for k in range(NWARM):
+
+        def spin():
             nc.tensor.matmul(warm[:], zeros[:, 0:P], zeros[:], start=True, stop=True)
+
+        for k in range(NWARM):
+            spin()
 
         ident = keep.tile([P, P], F32, name="ident")
         make_identity(nc, ident[:])
@@ -165,16 +169,20 @@ def tile_sparseconv2d_kernel(tc, inputs, kernel, out):
         regroup(0, "s", 0, H)
         regroup(1, "v", 0, H)
         weights_transpose(0)
+        spin()
         quantise_rows(0, 0, OD)
         quantise_rows(0, OD, H)
         weights_quantise(0)
         shift_scales(0)
         weights_transpose(2)
+        spin()
         weights_quantise(2)
         regroup(2, "v", 0, H)
         weights_transpose(4)
+        spin()
         weights_quantise(4)
         weights_transpose(6)
+        spin()
         weights_quantise(6)
         weights_transpose(8)
         regroup(3, "s", 0, H)

@@ -16,6 +16,7 @@ OA, OD = W - KH + 1, H - KW + 1
 GB = 2
 NG = B // GB
 ROW = GB * W
+LPITCH = 320
 N = OD * ROW
 NPASS = KH * KW
 NWARM = 4
@@ -70,11 +71,21 @@ def tile_sparseconv2d_kernel(tc, inputs, kernel, out):
         grp = keep.tile([P, NG, H * ROW * 4], BF16, name="grp", align_bytes=64)
         xcodes = keep.tile([P, NG, H * ROW], U32, name="xcodes", align_bytes=64)
         xshift = keep.tile([P, NG, N], U8, name="xshift", align_bytes=64)
+        lgrp = keep.tile([P, 2 * LPITCH * 4], BF16, name="lgrp", align_bytes=64)
+        lcodes = keep.tile([P, 2 * LPITCH], U32, name="lcodes", align_bytes=64)
+        lscales = keep.tile([P, KH, 2 * LPITCH], U8, name="lscales", align_bytes=64)
+        nc.gpsimd.memset(lscales[:, 0, :].bitcast(I32), 0)
+        for b in range(2):
+            nc.gpsimd.memset(lgrp[:, (b * LPITCH + H * W) * 4:(b + 1) * LPITCH * 4], 0.0)
         osb = keep.tile([P, NG, GB * OA * OD], F32, name="osb")
         banks = {}
 
         def regroup(b, engine, h0, h1):
-            dst = grp[:, b // GB, :].rearrange("p (h b w t) -> p h b w t", h=H, b=GB, w=W)[:, h0:h1, b % GB, :, :]
+            if b < B - GB:
+                dst = grp[:, b // GB, :].rearrange("p (h b w t) -> p h b w t", h=H, b=GB, w=W)[:, h0:h1, b % GB, :, :]
+            else:
+                c0 = (b % GB) * LPITCH
+                dst = lgrp[:, (c0 + h0 * W) * 4:(c0 + h1 * W) * 4].rearrange("p (h w t) -> p h w t", w=W, t=4)
             src = raw[:, b, :, h0 * W:h1 * W]
             if engine == "v":
                 nc.vector.tensor_copy(
@@ -93,6 +104,47 @@ def tile_sparseconv2d_kernel(tc, inputs, kernel, out):
 
         def shift_scales(g):
             nc.vector.tensor_copy(out=xshift[:, g, :].bitcast(I32), in_=xscales[:, g, ROW:ROW + N].bitcast(I32))
+
+        def quantise_last(c0, c1):
+            nc.vector.quantize_mx(
+                out=lcodes[:, c0:c1].bitcast(FP8X4),
+                scales=lscales[:, 0, c0:c1],
+                in_=lgrp[:, c0 * 4:c1 * 4],
+            )
+
+        def shift_last(j):
+            n = LPITCH + OD * W
+            nc.vector.tensor_copy(out=lscales[:, j, 0:n].bitcast(I32), in_=lscales[:, 0, j * W:j * W + n].bitcast(I32))
+
+        def last_multiply(b, i):
+            y = psum.tile([P, OD * W], F32, name="y", tag="bank")
+            banks[("last", b, i)] = y
+            for j in range(KW):
+                k = i * KW + j
+                c0 = b * LPITCH
+                nc.tensor.matmul_mx(
+                    out=y[:],
+                    lhsT=wcodes[:, k * F:(k + 1) * F].bitcast(FP8X4),
+                    lhsT_scale=wscales[:, k * F:(k + 1) * F],
+                    rhs=lcodes[:, c0 + j * W:c0 + j * W + OD * W].bitcast(FP8X4),
+                    rhs_scale=lscales[:, j, c0:c0 + OD * W],
+                    start=(j == 0),
+                    stop=(j == KW - 1),
+                )
+
+        def last_collect(b, i):
+            src = banks[("last", b, i)][:].rearrange("p (d w) -> p w d", d=OD)[:, i:i + OA, :]
+            dst = osb[:, NG - 1, :].rearrange("p (b a d) -> p b a d", b=GB, a=OA)[:, b, :, :]
+            if i == 0:
+                nc.scalar.copy(out=dst, in_=src)
+            else:
+                nc.vector.tensor_tensor(out=dst, in0=src, in1=dst, op=ADD)
+
+        def last_store(b):
+            nc.sync.dma_start(
+                out=out[B - GB + b].rearrange("f a d -> f (a d)"),
+                in_=osb[:, NG - 1, b * OA * OD:(b + 1) * OA * OD],
+            )
 
         def weights_transpose(g0, engine="s"):
             n = min(2, NPASS - g0)
@@ -185,8 +237,9 @@ def tile_sparseconv2d_kernel(tc, inputs, kernel, out):
         spin()
         weights_quantise(6)
         weights_transpose(8)
-        regroup(3, "s", 0, H)
+        regroup(3, "s", 6, H)
         weights_quantise(8)
+        regroup(3, "v", 0, 6)
         for i in range(KH):
             multiply(0, i)
 
@@ -208,22 +261,30 @@ def tile_sparseconv2d_kernel(tc, inputs, kernel, out):
         store(0)
 
         regroup(7, "s", 0, H)
-        quantise_rows(3, 0, OD)
-        quantise_rows(3, OD, H)
+        quantise_last(0, 512)
+        quantise_last(512, 2 * LPITCH)
         collect(1, 0)
-        shift_scales(3)
         collect(1, 1)
+        shift_last(1)
+        shift_last(2)
         collect(1, 2)
         store(1)
 
-        multiply(3, 0)
+        last_multiply(0, 0)
         collect(2, 0)
         collect(2, 1)
+        last_multiply(1, 0)
+        last_collect(0, 0)
+        last_multiply(0, 1)
+        last_collect(1, 0)
         collect(2, 2)
         store(2)
-        collect(3, 0)
-        for i in (1, 2):
-            for d0 in (0, 8):
-                multiply(3, i, d0, d0 + 8)
-                collect(3, i, d0, d0 + 8)
-        store(3)
+        last_multiply(1, 1)
+        last_collect(0, 1)
+        last_multiply(0, 2)
+        last_collect(1, 1)
+        last_multiply(1, 2)
+        last_collect(0, 2)
+        last_store(0)
+        last_collect(1, 2)
+        last_store(1)

@@ -58,8 +58,8 @@ def tile_sparseconv2d_kernel(tc, inputs, kernel, out):
         load_weights(2)
         load_weights(4)
         load_weights(6)
-        load_image(2)
         load_weights(8)
+        load_image(2)
         for b in range(3, B):
             load_image(b)
 
@@ -218,8 +218,10 @@ def tile_sparseconv2d_kernel(tc, inputs, kernel, out):
                 in_=osb[:, g, :].rearrange("p (b s) -> p b s", b=GB),
             )
 
-        regroup(0, "s", 0, H)
-        regroup(1, "v", 0, H)
+        regroup(0, "s", 10, H)
+        regroup(0, "v", 0, 10)
+        regroup(1, "s", 14, H)
+        regroup(1, "v", 0, 14)
         weights_transpose(0)
         spin()
         quantise_rows(0, 0, OD)

@@ -218,11 +218,12 @@ def tile_sparseconv2d_kernel(tc, inputs, kernel, out):
                 in_=osb[:, g, :].rearrange("p (b s) -> p b s", b=GB),
             )
 
-        regroup(0, "s", 10, H)
-        regroup(0, "v", 0, 10)
+        regroup(0, "s", 12, H)
+        regroup(0, "v", 0, 12)
         regroup(1, "s", 14, H)
         regroup(1, "v", 0, 14)
         weights_transpose(0)
+        spin()
         spin()
         quantise_rows(0, 0, OD)
         quantise_rows(0, OD, H)
@@ -239,9 +240,9 @@ def tile_sparseconv2d_kernel(tc, inputs, kernel, out):
         spin()
         weights_quantise(6)
         weights_transpose(8)
-        regroup(3, "s", 6, H)
+        regroup(3, "s", 8, H)
+        regroup(3, "v", 0, 8)
         weights_quantise(8)
-        regroup(3, "v", 0, 6)
         for i in range(KH):
             multiply(0, i)
 

@@ -58,8 +58,8 @@ def tile_sparseconv2d_kernel(tc, inputs, kernel, out):
         load_weights(2)
         load_weights(4)
         load_weights(6)
-        load_weights(8)
         load_image(2)
+        load_weights(8)
         for b in range(3, B):
             load_image(b)
 
@@ -237,11 +237,10 @@ def tile_sparseconv2d_kernel(tc, inputs, kernel, out):
         spin()
         weights_quantise(4)
         weights_transpose(6)
-        spin()
         weights_quantise(6)
         weights_transpose(8)
-        regroup(3, "s", 8, H)
-        regroup(3, "v", 0, 8)
+        regroup(3, "s", 10, H)
+        regroup(3, "v", 0, 10)
         weights_quantise(8)
         for i in range(KH):
             multiply(0, i)

import concourse.mybir as mybir
from concourse.masks import make_identity

F32 = mybir.dt.float32
BF16 = mybir.dt.bfloat16
I32 = mybir.dt.int32
U32 = mybir.dt.uint32
U8 = mybir.dt.uint8
FP8X4 = mybir.dt.float8_e4m3fn_x4
ADD = mybir.AluOpType.add

P = 128
B, C, H, W, F = 8, 512, 18, 16, 128
KH, KW = 3, 3
OA, OD = W - KH + 1, H - KW + 1
GB = 2
NG = B // GB
ROW = GB * W
LPITCH = 320
N = OD * ROW
NPASS = KH * KW
NWARM = 4

FLOPS = 2 * B * OA * OD * KH * KW * C * F


def tile_sparseconv2d_kernel(tc, inputs, kernel, out):
    nc = tc.nc
    with tc.tile_pool(name="keep", bufs=1) as keep, tc.psum_pool(name="psum", bufs=8) as psum, tc.manual_schedule():
        zeros = keep.tile([P, N], BF16, name="zeros")
        nc.vector.memset(zeros[:], 0.0)
        warm = psum.tile([P, N], F32, name="warm", tag="bank")

        def spin():
            nc.tensor.matmul(warm[:], zeros[:, 0:P], zeros[:], start=True, stop=True)

        for k in range(NWARM):
            spin()

        ident = keep.tile([P, P], F32, name="ident")
        make_identity(nc, ident[:])
        xscales = keep.tile([P, NG, H * ROW], U8, name="xscales", align_bytes=64)
        nc.vector.memset(xscales[:].rearrange("p g c -> p (g c)").bitcast(I32), 0)

        kw = keep.tile([P, NPASS * C], BF16, name="kw")
        raw = keep.tile([P, B, 4, H * W], BF16, name="raw")

        def load_image(b):
            nc.sync.dma_start(out=raw[:, b, :, :].rearrange("p t s -> p (t s)"), in_=inputs[b].rearrange("(p t) h w -> p (t h w)", t=4))

        def load_weights(g0):
            cols = slice(g0 * C, min(g0 + 2, NPASS) * C)
            nc.sync.dma_start(out=kw[:, cols], in_=kernel[:, cols])

        load_image(0)
        load_weights(0)
        load_image(1)
        load_weights(2)
        load_weights(4)
        load_weights(6)
        load_image(2)
        load_weights(8)
        for b in range(3, B):
            load_image(b)

        kwords = kw[:].bitcast(F32).rearrange("p (g q u) -> p g u q", q=P, u=2)
        wgrp = keep.tile([P, NPASS * 4 * F], BF16, name="wgrp", align_bytes=64)
        wgrp_words = wgrp[:].bitcast(F32).rearrange("p (g f u) -> p g f u", f=F, u=2)
        wcodes = keep.tile([P, NPASS * F], U32, name="wcodes", align_bytes=64)
        wscales = keep.tile([P, NPASS * F], U8, name="wscales", align_bytes=64)
        grp = keep.tile([P, NG, H * ROW * 4], BF16, name="grp", align_bytes=64)
        xcodes = keep.tile([P, NG, H * ROW], U32, name="xcodes", align_bytes=64)
        xshift = keep.tile([P, NG, N], U8, name="xshift", align_bytes=64)
        lgrp = keep.tile([P, 2 * LPITCH * 4], BF16, name="lgrp", align_bytes=64)
        lcodes = keep.tile([P, 2 * LPITCH], U32, name="lcodes", align_bytes=64)
        lscales = keep.tile([P, KH, 2 * LPITCH], U8, name="lscales", align_bytes=64)
        nc.gpsimd.memset(lscales[:, 0, :].bitcast(I32), 0)
        for b in range(2):
            nc.gpsimd.memset(lgrp[:, (b * LPITCH + H * W) * 4:(b + 1) * LPITCH * 4], 0.0)
        osb = keep.tile([P, NG, GB * OA * OD], F32, name="osb")
        banks = {}

        def regroup(b, engine, h0, h1):
            if b < B - GB:
                dst = grp[:, b // GB, :].rearrange("p (h b w t) -> p h b w t", h=H, b=GB, w=W)[:, h0:h1, b % GB, :, :]
            else:
                c0 = (b % GB) * LPITCH
                dst = lgrp[:, (c0 + h0 * W) * 4:(c0 + h1 * W) * 4].rearrange("p (h w t) -> p h w t", w=W, t=4)
            src = raw[:, b, :, h0 * W:h1 * W]
            if engine == "v":
                nc.vector.tensor_copy(
                    out=dst.rearrange("p h (q i) t -> p h q t i", i=4),
                    in_=src.rearrange("p t (h q i) -> p h q t i", q=4, i=4),
                )
            else:
                nc.scalar.copy(out=dst, in_=src.rearrange("p t (h w) -> p h w t", w=W))

        def quantise_rows(g, h0, h1):
            nc.vector.quantize_mx(
                out=xcodes[:, g, h0 * ROW:h1 * ROW].bitcast(FP8X4),
                scales=xscales[:, g, h0 * ROW:h1 * ROW],
                in_=grp[:, g, h0 * ROW * 4:h1 * ROW * 4],
            )

        def shift_scales(g):
            nc.vector.tensor_copy(out=xshift[:, g, :].bitcast(I32), in_=xscales[:, g, ROW:ROW + N].bitcast(I32))

        def quantise_last(c0, c1):
            nc.vector.quantize_mx(
                out=lcodes[:, c0:c1].bitcast(FP8X4),
                scales=lscales[:, 0, c0:c1],
                in_=lgrp[:, c0 * 4:c1 * 4],
            )

        def shift_last(j):
            n = LPITCH + OD * W
            nc.vector.tensor_copy(out=lscales[:, j, 0:n].bitcast(I32), in_=lscales[:, 0, j * W:j * W + n].bitcast(I32))

        def last_multiply(b, i):
            y = psum.tile([P, OD * W], F32, name="y", tag="bank")
            banks[("last", b, i)] = y
            for j in range(KW):
                k = i * KW + j
                c0 = b * LPITCH
                nc.tensor.matmul_mx(
                    out=y[:],
                    lhsT=wcodes[:, k * F:(k + 1) * F].bitcast(FP8X4),
                    lhsT_scale=wscales[:, k * F:(k + 1) * F],
                    rhs=lcodes[:, c0 + j * W:c0 + j * W + OD * W].bitcast(FP8X4),
                    rhs_scale=lscales[:, j, c0:c0 + OD * W],
                    start=(j == 0),
                    stop=(j == KW - 1),
                )

        def last_collect(b, i):
            src = banks[("last", b, i)][:].rearrange("p (d w) -> p w d", d=OD)[:, i:i + OA, :]
            dst = osb[:, NG - 1, :].rearrange("p (b a d) -> p b a d", b=GB, a=OA)[:, b, :, :]
            if i == 0:
                nc.scalar.copy(out=dst, in_=src)
            else:
                nc.vector.tensor_tensor(out=dst, in0=src, in1=dst, op=ADD)

        def last_store(b):
            nc.sync.dma_start(
                out=out[B - GB + b].rearrange("f a d -> f (a d)"),
                in_=osb[:, NG - 1, b * OA * OD:(b + 1) * OA * OD],
            )

        def weights_transpose(g0, engine="s"):
            n = min(2, NPASS - g0)
            wt = psum.tile([P, 2, 2, F], F32, name="wt", tag="bank")
            for k in range(n):
                for u in range(2):
                    nc.tensor.transpose(wt[:, k, u, :], kwords[:, g0 + k, u, :], ident[:])
            if engine == "s":
                nc.scalar.copy(out=wgrp_words[:, g0:g0 + n, :, :], in_=wt[:, 0:n, :, :].rearrange("p g u f -> p g f u"))
            else:
                nc.vector.tensor_copy(out=wgrp_words[:, g0:g0 + n, :, :], in_=wt[:, 0:n, :, :].rearrange("p g u f -> p g f u"))

        def weights_quantise(g0):
            n = min(2, NPASS - g0)
            nc.vector.quantize_mx(
                out=wcodes[:, g0 * F:(g0 + n) * F].bitcast(FP8X4),
                scales=wscales[:, g0 * F:(g0 + n) * F],
                in_=wgrp[:, g0 * 4 * F:(g0 + n) * 4 * F],
            )

        def one_pass(g, k, d0=0, d1=OD):
            i, j = divmod(k, KW)
            n = (d1 - d0) * ROW
            if j == 0:
                banks[(g, i, d0)] = psum.tile([P, n], F32, name="y", tag="bank")
            c0 = (d0 + j) * ROW
            plane = xshift[:, g, c0 - ROW:c0 - ROW + n] if j == 1 else xscales[:, g, c0:c0 + n]
            nc.tensor.matmul_mx(
                out=banks[(g, i, d0)][:],
                lhsT=wcodes[:, k * F:(k + 1) * F].bitcast(FP8X4),
                lhsT_scale=wscales[:, k * F:(k + 1) * F],
                rhs=xcodes[:, g, c0:c0 + n].bitcast(FP8X4),
                rhs_scale=plane,
                start=(j == 0),
                stop=(j == KW - 1),
            )

        def multiply(g, i, d0=0, d1=OD):
            for j in range(KW):
                one_pass(g, i * KW + j, d0, d1)

        def multiply_shift_major(g):
            ys = [psum.tile([P, N], F32, name="y%d" % i, tag="bank") for i in range(KH)]
            for j in range(KW):
                for i in range(KH):
                    banks[(g, i, 0)] = ys[i]
                    k = i * KW + j
                    c0 = j * ROW
                    plane = xshift[:, g, :] if j == 1 else xscales[:, g, c0:c0 + N]
                    nc.tensor.matmul_mx(
                        out=ys[i][:],
                        lhsT=wcodes[:, k * F:(k + 1) * F].bitcast(FP8X4),
                        lhsT_scale=wscales[:, k * F:(k + 1) * F],
                        rhs=xcodes[:, g, c0:c0 + N].bitcast(FP8X4),
                        rhs_scale=plane,
                        start=(j == 0),
                        stop=(j == KW - 1),
                    )

        def collect(g, i, d0=0, d1=OD):
            src = banks[(g, i, d0)][:].rearrange("p (d b w) -> p b w d", d=d1 - d0, b=GB)[:, :, i:i + OA, :]
            dst = osb[:, g, :].rearrange("p (b a d) -> p b a d", b=GB, a=OA)[:, :, :, d0:d1]
            if i == 0:
                nc.scalar.copy(out=dst, in_=src)
            else:
                nc.vector.tensor_tensor(out=dst, in0=src, in1=dst, op=ADD)

        def store(g):
            nc.sync.dma_start(
                out=out[g * GB:(g + 1) * GB].rearrange("b f a d -> f b (a d)"),
                in_=osb[:, g, :].rearrange("p (b s) -> p b s", b=GB),
            )

        regroup(0, "s", 12, H)
        regroup(0, "v", 0, 12)
        regroup(1, "s", 14, H)
        regroup(1, "v", 0, 14)
        weights_transpose(0)
        spin()
        spin()
        quantise_rows(0, 0, OD)
        quantise_rows(0, OD, H)
        weights_quantise(0)
        shift_scales(0)
        weights_transpose(2)
        spin()
        weights_quantise(2)
        regroup(2, "v", 0, H)
        weights_transpose(4)
        spin()
        weights_quantise(4)
        weights_transpose(6)
        weights_quantise(6)
        weights_transpose(8)
        regroup(3, "s", 10, H)
        regroup(3, "v", 0, 10)
        weights_quantise(8)
        for i in range(KH):
            multiply(0, i)

        quantise_rows(1, 0, OD)
        quantise_rows(1, OD, H)
        regroup(4, "v", 0, H)
        shift_scales(1)
        multiply_shift_major(1)

        regroup(5, "s", 0, H)
        collect(0, 0)
        regroup(6, "v", 0, H)
        quantise_rows(2, 0, OD)
        quantise_rows(2, OD, H)
        collect(0, 1)
        shift_scales(2)
        multiply_shift_major(2)
        collect(0, 2)
        store(0)

        regroup(7, "s", 0, H)
        quantise_last(0, 512)
        quantise_last(512, 2 * LPITCH)
        collect(1, 0)
        collect(1, 1)
        shift_last(1)
        shift_last(2)
        collect(1, 2)
        store(1)

        last_multiply(0, 0)
        collect(2, 0)
        collect(2, 1)
        last_multiply(1, 0)
        last_collect(0, 0)
        last_multiply(0, 1)
        last_collect(1, 0)
        collect(2, 2)
        store(2)
        last_multiply(1, 1)
        last_collect(0, 1)
        last_multiply(0, 2)
        last_collect(1, 1)
        last_multiply(1, 2)
        last_collect(0, 2)
        last_store(0)
        last_collect(1, 2)
        last_store(1)
